import numpy as np
import ml_dtypes


def mxq(x, axis, fmt="e4m3"):
    dtype, down = {"e4m3": (ml_dtypes.float8_e4m3fn, 7), "e5m2": (ml_dtypes.float8_e5m2, 14)}[fmt]
    v = np.moveaxis(np.asarray(x, np.float32).astype(ml_dtypes.bfloat16).astype(np.float64), axis, -1)
    blocks = v.reshape(v.shape[:-1] + (-1, 32))
    amax = np.abs(blocks).max(-1, keepdims=True)
    byte = np.maximum(np.where(amax > 0, np.frexp(amax)[1] - 1 + 127, 0) - down, 1)
    scale = np.exp2(byte - 127.0)
    codes = (blocks / scale).astype(np.float32).astype(dtype).astype(np.float64)
    return np.moveaxis((codes * scale).reshape(v.shape), -1, axis)


WIDE = False


def mx_kscale(k):
    if not WIDE:
        return np.ones(k)
    levels = np.array([10, -10, 5, -5, 0])
    a = np.random.permutation(np.resize(levels, k // 512 * 4)).reshape(k // 512, 4)
    idx = np.arange(k)
    return np.exp2(a[idx // 512, idx % 128 // 32])


BF16 = ml_dtypes.bfloat16


def bf(x):
    return np.asarray(x, np.float32).astype(BF16)


def f64(x):
    return np.asarray(x).astype(np.float64)


B, N, T, D, DO, H, E = 128, 2, 8, 512, 512, 8, 128
S = N * T


def sigmoid(v):
    return 1.0 / (1.0 + np.exp(-v))


def setup_inputs():
    r = np.random.standard_normal
    s = mx_kscale(D)
    return {
        "x": bf(r((B, S, D)) * s),
        "edge_features": bf(r((B, E))),
        "Wv": bf(r((D, DO)) / np.sqrt(D) / s[:, None]),
        "bv": bf(r(DO) * 0.3),
        "Wgate": bf(r((E, DO)) / np.sqrt(E)),
        "bgate": bf(r(DO) * 0.3),
        "Wscale": bf(r((E, DO)) * 0.7 / np.sqrt(E)),
        "bscale": bf(r(DO) * 0.3),
        "Wshift": bf(r((E, DO)) * 0.7 / np.sqrt(E)),
        "bshift": bf(r(DO) * 0.3),
    }


def reference(x, edge_features, Wv, bv, Wgate, bgate, Wscale, bscale, Wshift, bshift):
    e = f64(edge_features)
    v = (mxq(f64(x).reshape(B * S, D), 1, "e4m3") @ mxq(f64(Wv), 0, "e4m3")).reshape(B, S, DO) + f64(bv)
    gate = sigmoid(e @ f64(Wgate) + f64(bgate))
    scale = np.tanh(e @ f64(Wscale) + f64(bscale))
    shift = e @ f64(Wshift) + f64(bshift)
    return (v * (1.0 + scale[:, None, :]) + shift[:, None, :]) * gate[:, None, :]

@@ -1,0 +1,158 @@
+from contextlib import ExitStack
+
+import concourse.mybir as mybir
+from concourse.masks import make_identity
+
+F32 = mybir.dt.float32
+BF16 = mybir.dt.bfloat16
+U32 = mybir.dt.uint32
+U8 = mybir.dt.uint8
+FP8X4 = mybir.dt.float8_e4m3fn_x4
+ACT = mybir.ActivationFunctionType
+ALU = mybir.AluOpType
+
+P = 128
+B, S, D, DO, E = 128, 16, 512, 512, 128
+PACK = 4
+HALVES = 2
+ROWS = 2
+ROUNDS = S // ROWS
+CHUNKS = DO // P
+
+FLOPS = 2 * B * S * D * DO + 3 * 2 * B * E * DO
+
+
+def tile_graphditunit_pa_kernel(
+    tc, x, edge_features, Wv, bv, Wgate, bgate, Wscale, bscale, Wshift, bshift, out
+):
+    nc = tc.nc
+    with ExitStack() as ctx:
+        const = ctx.enter_context(tc.tile_pool(name="const", bufs=1))
+        per_round = ctx.enter_context(tc.tile_pool(name="per_round", bufs=ROUNDS))
+        psum_x = ctx.enter_context(tc.psum_pool(name="psum_x", bufs=2))
+        psum_acc = ctx.enter_context(tc.psum_pool(name="psum_acc", bufs=6))
+
+        e_sb = const.tile([P, E], BF16)
+        nc.sync.dma_start(out=e_sb[:], in_=edge_features)
+        w_mod = const.tile([P, 3, DO], BF16)
+        for j, w in enumerate((Wgate, Wscale, Wshift)):
+            nc.sync.dma_start(out=w_mod[:, j, :], in_=w)
+        w_raw = const.tile([P, PACK, DO], BF16)
+        nc.sync.dma_start(
+            out=w_raw[:].rearrange("p (u e) c -> p u (e c)", u=HALVES),
+            in_=Wv.rearrange("(u p e) c -> p u (e c)", u=HALVES, p=P),
+        )
+        x_tiles = []
+        for r in range(ROUNDS):
+            x_r = per_round.tile([P, ROWS * D], BF16)
+            nc.sync.dma_start(
+                out=x_r[:], in_=x[:, r * ROWS : (r + 1) * ROWS, :].rearrange("b i k -> b (i k)")
+            )
+            x_tiles.append(x_r)
+
+        bias_rows = const.tile([P, 3, DO], BF16)
+        nc.vector.memset(bias_rows[:], 0.0)
+        for j, bias in enumerate((bgate, bscale, bshift)):
+            nc.scalar.dma_start(
+                out=bias_rows[0:1, j, :], in_=bias.rearrange("(o c) -> o c", o=1)
+            )
+        bv_rows = const.tile([P, P], BF16)
+        nc.vector.memset(bv_rows[:], 0.0)
+        nc.scalar.dma_start(out=bv_rows[0:CHUNKS, :], in_=bv.rearrange("(c n) -> c n", n=P))
+
+        ident_bf16 = const.tile([P, P], BF16)
+        make_identity(nc, ident_bf16[:])
+        ident_f32 = const.tile([P, P], F32)
+        make_identity(nc, ident_f32[:])
+        ones = const.tile([P, P], BF16)
+        nc.vector.memset(ones[:], 1.0)
+        warm = const.tile([P, 1], F32)
+        nc.vector.memset(warm[:], 0.0)
+        nc.scalar.activation(out=warm[:], in_=warm[:], func=ACT.Sigmoid)
+
+        small_t = psum_acc.tile([P, 2, P], BF16, tag="acc")
+        nc.tensor.transpose(small_t[:, 0, :], e_sb[:], ident_bf16[:])
+        nc.tensor.transpose(small_t[:, 1, :], bv_rows[:], ident_bf16[:])
+        e_t = const.tile([P, B], BF16)
+        nc.vector.tensor_copy(out=e_t[:], in_=small_t[:, 0, :])
+        bv_t = const.tile([P, CHUNKS], F32)
+        nc.vector.tensor_copy(out=bv_t[:], in_=small_t[:, 1, 0:CHUNKS])
+        bv_rep = const.tile([P, CHUNKS, P], F32)
+        nc.vector.tensor_copy(out=bv_rep[:], in_=bv_t[:].unsqueeze(2).to_broadcast([P, CHUNKS, P]))
+        bv_all = psum_acc.tile([P, CHUNKS, P], F32, tag="acc")
+        for c in range(CHUNKS):
+            nc.tensor.transpose(bv_all[:, c, :], bv_rep[:, c, :], ident_f32[:])
+
+        pre = []
+        for j in range(3):
+            pre_j = psum_acc.tile([P, DO], F32, tag="acc")
+            nc.tensor.matmul(out=pre_j[:], lhsT=e_t[:], rhs=w_mod[:, j, :], start=True, stop=False)
+            nc.tensor.matmul(out=pre_j[:], lhsT=ones[:], rhs=bias_rows[:, j, :], start=False, stop=True)
+            pre.append(pre_j)
+        gate = const.tile([P, DO], F32)
+        nc.scalar.activation(out=gate[:], in_=pre[0][:], func=ACT.Sigmoid)
+        scale = const.tile([P, DO], F32)
+        nc.scalar.activation(out=scale[:], in_=pre[1][:], func=ACT.Tanh)
+        mul = const.tile([P, DO], F32)
+        nc.vector.scalar_tensor_tensor(
+            out=mul[:], in0=scale[:], scalar=1.0, in1=gate[:], op0=ALU.add, op1=ALU.mult
+        )
+        add = const.tile([P, DO], F32)
+        nc.vector.scalar_tensor_tensor(
+            out=add[:],
+            in0=scale[:],
+            scalar=1.0,
+            in1=bv_all[:].rearrange("p c n -> p (c n)"),
+            op0=ALU.add,
+            op1=ALU.mult,
+        )
+        nc.vector.tensor_tensor(out=add[:], in0=add[:], in1=pre[2][:], op=ALU.add)
+        nc.vector.tensor_tensor(out=add[:], in0=add[:], in1=gate[:], op=ALU.mult)
+
+        w_grouped = const.tile([P, DO, PACK], BF16, align_bytes=64)
+        nc.vector.tensor_copy(out=w_grouped[:], in_=w_raw[:].rearrange("p t c -> p c t"))
+        w_codes = const.tile([P, DO], U32, align_bytes=64)
+        w_scales = const.tile([P, DO], U8, align_bytes=64)
+        nc.vector.quantize_mx(
+            out=w_codes[:].bitcast(FP8X4),
+            scales=w_scales[:],
+            in_=w_grouped[:].rearrange("p c t -> p (c t)"),
+        )
+
+        for r in range(ROUNDS):
+            x_words = x_tiles[r][:].bitcast(F32)
+            x_t = psum_x.tile([P, ROWS, HALVES, B], F32)
+            for i in range(ROWS):
+                for u in range(HALVES):
+                    first = (i * HALVES + u) * P
+                    nc.tensor.transpose(x_t[:, i, u, :], x_words[:, first : first + P], ident_f32[:])
+            x_grouped = per_round.tile([P, ROWS * B * PACK], BF16, align_bytes=64)
+            nc.scalar.copy(
+                out=x_grouped[:].bitcast(F32).rearrange("p (i b u) -> p i b u", i=ROWS, u=HALVES),
+                in_=x_t[:].rearrange("p i u b -> p i b u"),
+            )
+            x_codes = per_round.tile([P, ROWS * B], U32, align_bytes=64)
+            x_scales = per_round.tile([P, ROWS * B], U8, align_bytes=64)
+            nc.vector.quantize_mx(out=x_codes[:].bitcast(FP8X4), scales=x_scales[:], in_=x_grouped[:])
+
+            o_r = per_round.tile([P, ROWS, DO], F32)
+            for i in range(ROWS):
+                samples = slice(i * B, (i + 1) * B)
+                acc = psum_acc.tile([P, DO], F32, tag="acc")
+                nc.tensor.matmul_mx(
+                    out=acc[:],
+                    lhsT=x_codes[:, samples].bitcast(FP8X4),
+                    lhsT_scale=x_scales[:, samples],
+                    rhs=w_codes[:].bitcast(FP8X4),
+                    rhs_scale=w_scales[:],
+                    start=True,
+                    stop=True,
+                )
+                nc.vector.tensor_tensor(out=o_r[:, i, :], in0=acc[:], in1=mul[:], op=ALU.mult)
+            nc.vector.tensor_tensor(
+                out=o_r[:],
+                in0=o_r[:],
+                in1=add[:].unsqueeze(1).to_broadcast([P, ROWS, DO]),
+                op=ALU.add,
+            )
+            nc.sync.dma_start(out=out[:, r * ROWS : (r + 1) * ROWS, :], in_=o_r[:])

@@ -149,10 +149,6 @@ def tile_graphditunit_pa_kernel(
                     stop=True,
                 )
                 nc.vector.tensor_tensor(out=o_r[:, i, :], in0=acc[:], in1=mul[:], op=ALU.mult)
-            nc.vector.tensor_tensor(
-                out=o_r[:],
-                in0=o_r[:],
-                in1=add[:].unsqueeze(1).to_broadcast([P, ROWS, DO]),
-                op=ALU.add,
-            )
+                adder = nc.gpsimd if i % 2 == 0 else nc.vector
+                adder.tensor_tensor(out=o_r[:, i, :], in0=o_r[:, i, :], in1=add[:], op=ALU.add)
             nc.sync.dma_start(out=out[:, r * ROWS : (r + 1) * ROWS, :], in_=o_r[:])

@@ -149,6 +149,5 @@ def tile_graphditunit_pa_kernel(
                     stop=True,
                 )
                 nc.vector.tensor_tensor(out=o_r[:, i, :], in0=acc[:], in1=mul[:], op=ALU.mult)
-                adder = nc.gpsimd if i % 2 == 0 else nc.vector
-                adder.tensor_tensor(out=o_r[:, i, :], in0=o_r[:, i, :], in1=add[:], op=ALU.add)
+                nc.gpsimd.tensor_tensor(out=o_r[:, i, :], in0=o_r[:, i, :], in1=add[:], op=ALU.add)
             nc.sync.dma_start(out=out[:, r * ROWS : (r + 1) * ROWS, :], in_=o_r[:])

@@ -27,21 +27,45 @@ def tile_graphditunit_pa_kernel(
 ):
     nc = tc.nc
     with ExitStack() as ctx:
+        ctx.enter_context(tc.manual_schedule())
         const = ctx.enter_context(tc.tile_pool(name="const", bufs=1))
         per_round = ctx.enter_context(tc.tile_pool(name="per_round", bufs=ROUNDS))
+        per_row = ctx.enter_context(tc.tile_pool(name="per_row", bufs=S))
         psum_x = ctx.enter_context(tc.psum_pool(name="psum_x", bufs=2))
-        psum_acc = ctx.enter_context(tc.psum_pool(name="psum_acc", bufs=6))
+        psum_add = ctx.enter_context(tc.psum_pool(name="psum_add", bufs=1))
+        psum_acc = ctx.enter_context(tc.psum_pool(name="psum_acc", bufs=5))
+
+        ident_bf16 = const.tile([P, P], BF16)
+        make_identity(nc, ident_bf16[:])
+        ident_f32 = const.tile([P, P], F32)
+        make_identity(nc, ident_f32[:])
+        bias_rows = const.tile([P, 3, DO], BF16)
+        nc.vector.memset(bias_rows[:], 0.0)
+        bv_rows = const.tile([P, P], BF16)
+        nc.vector.memset(bv_rows[:], 0.0)
+        ones = const.tile([P, P], BF16)
+        nc.vector.memset(ones[:], 1.0)
+        warm = const.tile([P, 1], F32)
+        nc.vector.memset(warm[:], 0.0)
+
+        for j, bias in enumerate((bgate, bscale, bshift)):
+            nc.scalar.dma_start(
+                out=bias_rows[0:1, j, :], in_=bias.rearrange("(o c) -> o c", o=1)
+            )
+        nc.scalar.dma_start(out=bv_rows[0:CHUNKS, :], in_=bv.rearrange("(c n) -> c n", n=P))
+        nc.scalar.activation(out=warm[:], in_=warm[:], func=ACT.Sigmoid)
 
         e_sb = const.tile([P, E], BF16)
         nc.sync.dma_start(out=e_sb[:], in_=edge_features)
         w_mod = const.tile([P, 3, DO], BF16)
-        for j, w in enumerate((Wgate, Wscale, Wshift)):
-            nc.sync.dma_start(out=w_mod[:, j, :], in_=w)
+        nc.sync.dma_start(out=w_mod[:, 0, :], in_=Wgate)
+        nc.sync.dma_start(out=w_mod[:, 1, :], in_=Wscale)
         w_raw = const.tile([P, PACK, DO], BF16)
         nc.sync.dma_start(
             out=w_raw[:].rearrange("p (u e) c -> p u (e c)", u=HALVES),
             in_=Wv.rearrange("(u p e) c -> p u (e c)", u=HALVES, p=P),
         )
+        nc.sync.dma_start(out=w_mod[:, 2, :], in_=Wshift)
         x_tiles = []
         for r in range(ROUNDS):
             x_r = per_round.tile([P, ROWS * D], BF16)
@@ -49,26 +73,6 @@ def tile_graphditunit_pa_kernel(
                 out=x_r[:], in_=x[:, r * ROWS : (r + 1) * ROWS, :].rearrange("b i k -> b (i k)")
             )
             x_tiles.append(x_r)
-
-        bias_rows = const.tile([P, 3, DO], BF16)
-        nc.vector.memset(bias_rows[:], 0.0)
-        for j, bias in enumerate((bgate, bscale, bshift)):
-            nc.scalar.dma_start(
-                out=bias_rows[0:1, j, :], in_=bias.rearrange("(o c) -> o c", o=1)
-            )
-        bv_rows = const.tile([P, P], BF16)
-        nc.vector.memset(bv_rows[:], 0.0)
-        nc.scalar.dma_start(out=bv_rows[0:CHUNKS, :], in_=bv.rearrange("(c n) -> c n", n=P))
-
-        ident_bf16 = const.tile([P, P], BF16)
-        make_identity(nc, ident_bf16[:])
-        ident_f32 = const.tile([P, P], F32)
-        make_identity(nc, ident_f32[:])
-        ones = const.tile([P, P], BF16)
-        nc.vector.memset(ones[:], 1.0)
-        warm = const.tile([P, 1], F32)
-        nc.vector.memset(warm[:], 0.0)
-        nc.scalar.activation(out=warm[:], in_=warm[:], func=ACT.Sigmoid)
 
         small_t = psum_acc.tile([P, 2, P], BF16, tag="acc")
         nc.tensor.transpose(small_t[:, 0, :], e_sb[:], ident_bf16[:])
@@ -79,35 +83,23 @@ def tile_graphditunit_pa_kernel(
         nc.vector.tensor_copy(out=bv_t[:], in_=small_t[:, 1, 0:CHUNKS])
         bv_rep = const.tile([P, CHUNKS, P], F32)
         nc.vector.tensor_copy(out=bv_rep[:], in_=bv_t[:].unsqueeze(2).to_broadcast([P, CHUNKS, P]))
-        bv_all = psum_acc.tile([P, CHUNKS, P], F32, tag="acc")
-        for c in range(CHUNKS):
-            nc.tensor.transpose(bv_all[:, c, :], bv_rep[:, c, :], ident_f32[:])
 
-        pre = []
-        for j in range(3):
+        def edge_matmul(j):
             pre_j = psum_acc.tile([P, DO], F32, tag="acc")
             nc.tensor.matmul(out=pre_j[:], lhsT=e_t[:], rhs=w_mod[:, j, :], start=True, stop=False)
             nc.tensor.matmul(out=pre_j[:], lhsT=ones[:], rhs=bias_rows[:, j, :], start=False, stop=True)
-            pre.append(pre_j)
+            return pre_j
+
+        pre_gate = edge_matmul(0)
         gate = const.tile([P, DO], F32)
-        nc.scalar.activation(out=gate[:], in_=pre[0][:], func=ACT.Sigmoid)
+        nc.scalar.activation(out=gate[:], in_=pre_gate[:], func=ACT.Sigmoid)
+        pre_scale = edge_matmul(1)
         scale = const.tile([P, DO], F32)
-        nc.scalar.activation(out=scale[:], in_=pre[1][:], func=ACT.Tanh)
-        mul = const.tile([P, DO], F32)
-        nc.vector.scalar_tensor_tensor(
-            out=mul[:], in0=scale[:], scalar=1.0, in1=gate[:], op0=ALU.add, op1=ALU.mult
-        )
-        add = const.tile([P, DO], F32)
-        nc.vector.scalar_tensor_tensor(
-            out=add[:],
-            in0=scale[:],
-            scalar=1.0,
-            in1=bv_all[:].rearrange("p c n -> p (c n)"),
-            op0=ALU.add,
-            op1=ALU.mult,
-        )
-        nc.vector.tensor_tensor(out=add[:], in0=add[:], in1=pre[2][:], op=ALU.add)
-        nc.vector.tensor_tensor(out=add[:], in0=add[:], in1=gate[:], op=ALU.mult)
+        nc.scalar.activation(out=scale[:], in_=pre_scale[:], func=ACT.Tanh)
+        shift = edge_matmul(2)
+        bv_all = psum_acc.tile([P, CHUNKS, P], F32, tag="acc")
+        for c in range(CHUNKS):
+            nc.tensor.transpose(bv_all[:, c, :], bv_rep[:, c, :], ident_f32[:])
 
         w_grouped = const.tile([P, DO, PACK], BF16, align_bytes=64)
         nc.vector.tensor_copy(out=w_grouped[:], in_=w_raw[:].rearrange("p t c -> p c t"))
@@ -119,6 +111,20 @@ def tile_graphditunit_pa_kernel(
             in_=w_grouped[:].rearrange("p c t -> p (c t)"),
         )
 
+        mul = const.tile([P, DO], F32)
+        nc.vector.scalar_tensor_tensor(
+            out=mul[:], in0=scale[:], scalar=1.0, in1=gate[:], op0=ALU.add, op1=ALU.mult
+        )
+        shift_gate = const.tile([P, DO], F32)
+        nc.vector.tensor_tensor(out=shift_gate[:], in0=shift[:], in1=gate[:], op=ALU.mult)
+        add = const.tile([P, DO], F32)
+        nc.vector.tensor_tensor(
+            out=add[:], in0=bv_all[:].rearrange("p c n -> p (c n)"), in1=mul[:], op=ALU.mult
+        )
+        nc.vector.tensor_tensor(out=add[:], in0=add[:], in1=shift_gate[:], op=ALU.add)
+
+        x_codes = []
+        x_scales = []
         for r in range(ROUNDS):
             x_words = x_tiles[r][:].bitcast(F32)
             x_t = psum_x.tile([P, ROWS, HALVES, B], F32)
@@ -131,23 +137,52 @@ def tile_graphditunit_pa_kernel(
                 out=x_grouped[:].bitcast(F32).rearrange("p (i b u) -> p i b u", i=ROWS, u=HALVES),
                 in_=x_t[:].rearrange("p i u b -> p i b u"),
             )
-            x_codes = per_round.tile([P, ROWS * B], U32, align_bytes=64)
-            x_scales = per_round.tile([P, ROWS * B], U8, align_bytes=64)
-            nc.vector.quantize_mx(out=x_codes[:].bitcast(FP8X4), scales=x_scales[:], in_=x_grouped[:])
+            codes_r = per_round.tile([P, ROWS * B], U32, align_bytes=64)
+            scales_r = per_round.tile([P, ROWS * B], U8, align_bytes=64)
+            nc.vector.quantize_mx(out=codes_r[:].bitcast(FP8X4), scales=scales_r[:], in_=x_grouped[:])
+            x_codes.append(codes_r)
+            x_scales.append(scales_r)
 
-            o_r = per_round.tile([P, ROWS, DO], F32)
-            for i in range(ROWS):
-                samples = slice(i * B, (i + 1) * B)
-                acc = psum_acc.tile([P, DO], F32, tag="acc")
-                nc.tensor.matmul_mx(
-                    out=acc[:],
-                    lhsT=x_codes[:, samples].bitcast(FP8X4),
-                    lhsT_scale=x_scales[:, samples],
-                    rhs=w_codes[:].bitcast(FP8X4),
-                    rhs_scale=w_scales[:],
-                    start=True,
-                    stop=True,
+        add_t_psum = psum_acc.tile([P, CHUNKS, B], F32, tag="acc")
+        for c in range(CHUNKS):
+            nc.tensor.transpose(add_t_psum[:, c, :], add[:, c * P : (c + 1) * P], ident_f32[:])
+        add_t = const.tile([P, CHUNKS, B], F32)
+        nc.scalar.copy(out=add_t[:], in_=add_t_psum[:])
+        add_psum = psum_add.tile([P, CHUNKS, P], F32)
+        for c in range(CHUNKS):
+            nc.tensor.transpose(add_psum[:, c, :], add_t[:, c, :], ident_f32[:])
+
+        products = []
+
+        def multiply(i):
+            r = i // ROWS
+            samples = slice((i % ROWS) * B, (i % ROWS + 1) * B)
+            acc = psum_acc.tile([P, DO], F32, tag="acc")
+            nc.tensor.matmul_mx(
+                out=acc[:],
+                lhsT=x_codes[r][:, samples].bitcast(FP8X4),
+                lhsT_scale=x_scales[r][:, samples],
+                rhs=w_codes[:].bitcast(FP8X4),
+                rhs_scale=w_scales[:],
+                start=True,
+                stop=True,
+            )
+            o_i = per_row.tile([P, DO], F32)
+            nc.vector.tensor_tensor(out=o_i[:], in0=acc[:], in1=mul[:], op=ALU.mult)
+            products.append(o_i)
+
+        def add_and_store(i):
+            o_i = products[i]
+            if i % 2 == 0:
+                nc.gpsimd.tensor_tensor(out=o_i[:], in0=o_i[:], in1=add[:], op=ALU.add)
+            else:
+                nc.vector.tensor_tensor(
+                    out=o_i[:], in0=o_i[:], in1=add_psum[:].rearrange("p c n -> p (c n)"), op=ALU.add
                 )
-                nc.vector.tensor_tensor(out=o_r[:, i, :], in0=acc[:], in1=mul[:], op=ALU.mult)
-                nc.gpsimd.tensor_tensor(out=o_r[:, i, :], in0=o_r[:, i, :], in1=add[:], op=ALU.add)
-            nc.sync.dma_start(out=out[:, r * ROWS : (r + 1) * ROWS, :], in_=o_r[:])
+            nc.sync.dma_start(out=out[:, i, :], in_=o_i[:])
+
+        for i in range(S):
+            multiply(i)
+            if i > 0:
+                add_and_store(i - 1)
+        add_and_store(S - 1)

@@ -18,6 +18,8 @@ HALVES = 2
 ROWS = 2
 ROUNDS = S // ROWS
 CHUNKS = DO // P
+EARLY_ROUNDS = 2
+ADD_LAG = 3
 
 FLOPS = 2 * B * S * D * DO + 3 * 2 * B * E * DO
 
@@ -31,28 +33,26 @@ def tile_graphditunit_pa_kernel(
         const = ctx.enter_context(tc.tile_pool(name="const", bufs=1))
         per_round = ctx.enter_context(tc.tile_pool(name="per_round", bufs=ROUNDS))
         per_row = ctx.enter_context(tc.tile_pool(name="per_row", bufs=S))
-        psum_x = ctx.enter_context(tc.psum_pool(name="psum_x", bufs=2))
         psum_add = ctx.enter_context(tc.psum_pool(name="psum_add", bufs=1))
-        psum_acc = ctx.enter_context(tc.psum_pool(name="psum_acc", bufs=5))
+        psum = ctx.enter_context(tc.psum_pool(name="psum", bufs=7))
 
         ident_bf16 = const.tile([P, P], BF16)
         make_identity(nc, ident_bf16[:])
         ident_f32 = const.tile([P, P], F32)
         make_identity(nc, ident_f32[:])
-        bias_rows = const.tile([P, 3, DO], BF16)
-        nc.vector.memset(bias_rows[:], 0.0)
         bv_rows = const.tile([P, P], BF16)
         nc.vector.memset(bv_rows[:], 0.0)
+        nc.scalar.dma_start(out=bv_rows[0:CHUNKS, :], in_=bv.rearrange("(c n) -> c n", n=P))
+        bias_planes = []
+        for bias in (bgate, bscale, bshift):
+            plane = const.tile([P, DO], BF16, tag="plane", bufs=3)
+            nc.vector.memset(plane[:], 0.0)
+            nc.scalar.dma_start(out=plane[0:1, :], in_=bias.rearrange("(o c) -> o c", o=1))
+            bias_planes.append(plane)
         ones = const.tile([P, P], BF16)
         nc.vector.memset(ones[:], 1.0)
         warm = const.tile([P, 1], F32)
         nc.vector.memset(warm[:], 0.0)
-
-        for j, bias in enumerate((bgate, bscale, bshift)):
-            nc.scalar.dma_start(
-                out=bias_rows[0:1, j, :], in_=bias.rearrange("(o c) -> o c", o=1)
-            )
-        nc.scalar.dma_start(out=bv_rows[0:CHUNKS, :], in_=bv.rearrange("(c n) -> c n", n=P))
         nc.scalar.activation(out=warm[:], in_=warm[:], func=ACT.Sigmoid)
 
         e_sb = const.tile([P, E], BF16)
@@ -74,7 +74,7 @@ def tile_graphditunit_pa_kernel(
             )
             x_tiles.append(x_r)
 
-        small_t = psum_acc.tile([P, 2, P], BF16, tag="acc")
+        small_t = psum.tile([P, 2, P], BF16, tag="bank")
         nc.tensor.transpose(small_t[:, 0, :], e_sb[:], ident_bf16[:])
         nc.tensor.transpose(small_t[:, 1, :], bv_rows[:], ident_bf16[:])
         e_t = const.tile([P, B], BF16)
@@ -85,9 +85,9 @@ def tile_graphditunit_pa_kernel(
         nc.vector.tensor_copy(out=bv_rep[:], in_=bv_t[:].unsqueeze(2).to_broadcast([P, CHUNKS, P]))
 
         def edge_matmul(j):
-            pre_j = psum_acc.tile([P, DO], F32, tag="acc")
+            pre_j = psum.tile([P, DO], F32, tag="bank")
             nc.tensor.matmul(out=pre_j[:], lhsT=e_t[:], rhs=w_mod[:, j, :], start=True, stop=False)
-            nc.tensor.matmul(out=pre_j[:], lhsT=ones[:], rhs=bias_rows[:, j, :], start=False, stop=True)
+            nc.tensor.matmul(out=pre_j[:], lhsT=ones[:], rhs=bias_planes[j][:], start=False, stop=True)
             return pre_j
 
         pre_gate = edge_matmul(0)
@@ -96,10 +96,6 @@ def tile_graphditunit_pa_kernel(
         pre_scale = edge_matmul(1)
         scale = const.tile([P, DO], F32)
         nc.scalar.activation(out=scale[:], in_=pre_scale[:], func=ACT.Tanh)
-        shift = edge_matmul(2)
-        bv_all = psum_acc.tile([P, CHUNKS, P], F32, tag="acc")
-        for c in range(CHUNKS):
-            nc.tensor.transpose(bv_all[:, c, :], bv_rep[:, c, :], ident_f32[:])
 
         w_grouped = const.tile([P, DO, PACK], BF16, align_bytes=64)
         nc.vector.tensor_copy(out=w_grouped[:], in_=w_raw[:].rearrange("p t c -> p c t"))
@@ -111,6 +107,29 @@ def tile_graphditunit_pa_kernel(
             in_=w_grouped[:].rearrange("p c t -> p (c t)"),
         )
 
+        x_grouped = []
+
+        def transpose_x(r):
+            x_words = x_tiles[r][:].bitcast(F32)
+            x_t = psum.tile([P, ROWS, HALVES, B], F32, tag="bank")
+            for i in range(ROWS):
+                for u in range(HALVES):
+                    first = (i * HALVES + u) * P
+                    nc.tensor.transpose(x_t[:, i, u, :], x_words[:, first : first + P], ident_f32[:])
+            grouped_r = per_round.tile([P, ROWS * B * PACK], BF16, align_bytes=64)
+            nc.scalar.copy(
+                out=grouped_r[:].bitcast(F32).rearrange("p (i b u) -> p i b u", i=ROWS, u=HALVES),
+                in_=x_t[:].rearrange("p i u b -> p i b u"),
+            )
+            x_grouped.append(grouped_r)
+
+        for r in range(EARLY_ROUNDS):
+            transpose_x(r)
+
+        shift = edge_matmul(2)
+        bv_all = psum.tile([P, CHUNKS, P], F32, tag="bank")
+        for c in range(CHUNKS):
+            nc.tensor.transpose(bv_all[:, c, :], bv_rep[:, c, :], ident_f32[:])
         mul = const.tile([P, DO], F32)
         nc.vector.scalar_tensor_tensor(
             out=mul[:], in0=scale[:], scalar=1.0, in1=gate[:], op0=ALU.add, op1=ALU.mult
@@ -123,41 +142,32 @@ def tile_graphditunit_pa_kernel(
         )
         nc.vector.tensor_tensor(out=add[:], in0=add[:], in1=shift_gate[:], op=ALU.add)
 
+        for r in range(EARLY_ROUNDS, ROUNDS):
+            transpose_x(r)
+
         x_codes = []
         x_scales = []
         for r in range(ROUNDS):
-            x_words = x_tiles[r][:].bitcast(F32)
-            x_t = psum_x.tile([P, ROWS, HALVES, B], F32)
-            for i in range(ROWS):
-                for u in range(HALVES):
-                    first = (i * HALVES + u) * P
-                    nc.tensor.transpose(x_t[:, i, u, :], x_words[:, first : first + P], ident_f32[:])
-            x_grouped = per_round.tile([P, ROWS * B * PACK], BF16, align_bytes=64)
-            nc.scalar.copy(
-                out=x_grouped[:].bitcast(F32).rearrange("p (i b u) -> p i b u", i=ROWS, u=HALVES),
-                in_=x_t[:].rearrange("p i u b -> p i b u"),
-            )
             codes_r = per_round.tile([P, ROWS * B], U32, align_bytes=64)
             scales_r = per_round.tile([P, ROWS * B], U8, align_bytes=64)
-            nc.vector.quantize_mx(out=codes_r[:].bitcast(FP8X4), scales=scales_r[:], in_=x_grouped[:])
+            nc.vector.quantize_mx(
+                out=codes_r[:].bitcast(FP8X4), scales=scales_r[:], in_=x_grouped[r][:]
+            )
             x_codes.append(codes_r)
             x_scales.append(scales_r)
 
-        add_t_psum = psum_acc.tile([P, CHUNKS, B], F32, tag="acc")
+        add_t_psum = psum.tile([P, CHUNKS, B], F32, tag="bank")
         for c in range(CHUNKS):
             nc.tensor.transpose(add_t_psum[:, c, :], add[:, c * P : (c + 1) * P], ident_f32[:])
         add_t = const.tile([P, CHUNKS, B], F32)
         nc.scalar.copy(out=add_t[:], in_=add_t_psum[:])
-        add_psum = psum_add.tile([P, CHUNKS, P], F32)
-        for c in range(CHUNKS):
-            nc.tensor.transpose(add_psum[:, c, :], add_t[:, c, :], ident_f32[:])
 
         products = []
 
         def multiply(i):
             r = i // ROWS
             samples = slice((i % ROWS) * B, (i % ROWS + 1) * B)
-            acc = psum_acc.tile([P, DO], F32, tag="acc")
+            acc = psum.tile([P, DO], F32, tag="bank")
             nc.tensor.matmul_mx(
                 out=acc[:],
                 lhsT=x_codes[r][:, samples].bitcast(FP8X4),
@@ -181,8 +191,13 @@ def tile_graphditunit_pa_kernel(
                 )
             nc.sync.dma_start(out=out[:, i, :], in_=o_i[:])
 
-        for i in range(S):
+        for i in range(ADD_LAG):
             multiply(i)
-            if i > 0:
-                add_and_store(i - 1)
-        add_and_store(S - 1)
+        add_psum = psum_add.tile([P, CHUNKS, P], F32)
+        for c in range(CHUNKS):
+            nc.tensor.transpose(add_psum[:, c, :], add_t[:, c, :], ident_f32[:])
+        for i in range(ADD_LAG, S):
+            multiply(i)
+            add_and_store(i - ADD_LAG)
+        for i in range(S - ADD_LAG, S):
+            add_and_store(i)

@@ -18,6 +18,7 @@ HALVES = 2
 ROWS = 2
 ROUNDS = S // ROWS
 CHUNKS = DO // P
+RUN = 4
 EARLY_ROUNDS = 2
 ADD_LAG = 3
 
@@ -74,31 +75,37 @@ def tile_graphditunit_pa_kernel(
             )
             x_tiles.append(x_r)
 
+        def edge_product(j):
+            pre_j = psum.tile([P, DO], F32, tag="bank")
+            nc.tensor.matmul(out=pre_j[:], lhsT=e_t[:], rhs=w_mod[:, j, :], start=True, stop=False)
+            return pre_j
+
+        def add_bias(pre_j, j):
+            nc.tensor.matmul(out=pre_j[:], lhsT=ones[:], rhs=bias_planes[j][:], start=False, stop=True)
+
         small_t = psum.tile([P, 2, P], BF16, tag="bank")
         nc.tensor.transpose(small_t[:, 0, :], e_sb[:], ident_bf16[:])
-        nc.tensor.transpose(small_t[:, 1, :], bv_rows[:], ident_bf16[:])
         e_t = const.tile([P, B], BF16)
         nc.vector.tensor_copy(out=e_t[:], in_=small_t[:, 0, :])
+        pre_gate = edge_product(0)
+        pre_scale = edge_product(1)
+        nc.tensor.transpose(small_t[:, 1, :], bv_rows[:], ident_bf16[:])
         bv_t = const.tile([P, CHUNKS], F32)
         nc.vector.tensor_copy(out=bv_t[:], in_=small_t[:, 1, 0:CHUNKS])
         bv_rep = const.tile([P, CHUNKS, P], F32)
         nc.vector.tensor_copy(out=bv_rep[:], in_=bv_t[:].unsqueeze(2).to_broadcast([P, CHUNKS, P]))
-
-        def edge_matmul(j):
-            pre_j = psum.tile([P, DO], F32, tag="bank")
-            nc.tensor.matmul(out=pre_j[:], lhsT=e_t[:], rhs=w_mod[:, j, :], start=True, stop=False)
-            nc.tensor.matmul(out=pre_j[:], lhsT=ones[:], rhs=bias_planes[j][:], start=False, stop=True)
-            return pre_j
-
-        pre_gate = edge_matmul(0)
+        add_bias(pre_gate, 0)
         gate = const.tile([P, DO], F32)
         nc.scalar.activation(out=gate[:], in_=pre_gate[:], func=ACT.Sigmoid)
-        pre_scale = edge_matmul(1)
+        add_bias(pre_scale, 1)
         scale = const.tile([P, DO], F32)
         nc.scalar.activation(out=scale[:], in_=pre_scale[:], func=ACT.Tanh)
 
         w_grouped = const.tile([P, DO, PACK], BF16, align_bytes=64)
-        nc.vector.tensor_copy(out=w_grouped[:], in_=w_raw[:].rearrange("p t c -> p c t"))
+        nc.vector.tensor_copy(
+            out=w_grouped[:].rearrange("p (c i) t -> p c t i", i=RUN),
+            in_=w_raw[:].rearrange("p t (c i) -> p c t i", i=RUN),
+        )
         w_codes = const.tile([P, DO], U32, align_bytes=64)
         w_scales = const.tile([P, DO], U8, align_bytes=64)
         nc.vector.quantize_mx(
@@ -126,7 +133,8 @@ def tile_graphditunit_pa_kernel(
         for r in range(EARLY_ROUNDS):
             transpose_x(r)
 
-        shift = edge_matmul(2)
+        shift = edge_product(2)
+        add_bias(shift, 2)
         bv_all = psum.tile([P, CHUNKS, P], F32, tag="bank")
         for c in range(CHUNKS):
             nc.tensor.transpose(bv_all[:, c, :], bv_rep[:, c, :], ident_f32[:])
@@ -140,14 +148,11 @@ def tile_graphditunit_pa_kernel(
         nc.vector.tensor_tensor(
             out=add[:], in0=bv_all[:].rearrange("p c n -> p (c n)"), in1=mul[:], op=ALU.mult
         )
-        nc.vector.tensor_tensor(out=add[:], in0=add[:], in1=shift_gate[:], op=ALU.add)
-
-        for r in range(EARLY_ROUNDS, ROUNDS):
-            transpose_x(r)
 
         x_codes = []
         x_scales = []
-        for r in range(ROUNDS):
+
+        def quantise_x(r):
             codes_r = per_round.tile([P, ROWS * B], U32, align_bytes=64)
             scales_r = per_round.tile([P, ROWS * B], U8, align_bytes=64)
             nc.vector.quantize_mx(
@@ -155,6 +160,14 @@ def tile_graphditunit_pa_kernel(
             )
             x_codes.append(codes_r)
             x_scales.append(scales_r)
+
+        quantise_x(0)
+        nc.vector.tensor_tensor(out=add[:], in0=add[:], in1=shift_gate[:], op=ALU.add)
+
+        for r in range(EARLY_ROUNDS, ROUNDS):
+            transpose_x(r)
+        for r in range(1, ROUNDS):
+            quantise_x(r)
 
         add_t_psum = psum.tile([P, CHUNKS, B], F32, tag="bank")
         for c in range(CHUNKS):

@@ -75,29 +75,26 @@ def tile_graphditunit_pa_kernel(
             )
             x_tiles.append(x_r)
 
-        def edge_product(j):
-            pre_j = psum.tile([P, DO], F32, tag="bank")
-            nc.tensor.matmul(out=pre_j[:], lhsT=e_t[:], rhs=w_mod[:, j, :], start=True, stop=False)
-            return pre_j
-
-        def add_bias(pre_j, j):
-            nc.tensor.matmul(out=pre_j[:], lhsT=ones[:], rhs=bias_planes[j][:], start=False, stop=True)
-
         small_t = psum.tile([P, 2, P], BF16, tag="bank")
         nc.tensor.transpose(small_t[:, 0, :], e_sb[:], ident_bf16[:])
+        nc.tensor.transpose(small_t[:, 1, :], bv_rows[:], ident_bf16[:])
         e_t = const.tile([P, B], BF16)
         nc.vector.tensor_copy(out=e_t[:], in_=small_t[:, 0, :])
-        pre_gate = edge_product(0)
-        pre_scale = edge_product(1)
-        nc.tensor.transpose(small_t[:, 1, :], bv_rows[:], ident_bf16[:])
         bv_t = const.tile([P, CHUNKS], F32)
         nc.vector.tensor_copy(out=bv_t[:], in_=small_t[:, 1, 0:CHUNKS])
         bv_rep = const.tile([P, CHUNKS, P], F32)
         nc.vector.tensor_copy(out=bv_rep[:], in_=bv_t[:].unsqueeze(2).to_broadcast([P, CHUNKS, P]))
-        add_bias(pre_gate, 0)
+
+        def edge_matmul(j):
+            pre_j = psum.tile([P, DO], F32, tag="bank")
+            nc.tensor.matmul(out=pre_j[:], lhsT=e_t[:], rhs=w_mod[:, j, :], start=True, stop=False)
+            nc.tensor.matmul(out=pre_j[:], lhsT=ones[:], rhs=bias_planes[j][:], start=False, stop=True)
+            return pre_j
+
+        pre_gate = edge_matmul(0)
         gate = const.tile([P, DO], F32)
         nc.scalar.activation(out=gate[:], in_=pre_gate[:], func=ACT.Sigmoid)
-        add_bias(pre_scale, 1)
+        pre_scale = edge_matmul(1)
         scale = const.tile([P, DO], F32)
         nc.scalar.activation(out=scale[:], in_=pre_scale[:], func=ACT.Tanh)
 
@@ -133,8 +130,7 @@ def tile_graphditunit_pa_kernel(
         for r in range(EARLY_ROUNDS):
             transpose_x(r)
 
-        shift = edge_product(2)
-        add_bias(shift, 2)
+        shift = edge_matmul(2)
         bv_all = psum.tile([P, CHUNKS, P], F32, tag="bank")
         for c in range(CHUNKS):
             nc.tensor.transpose(bv_all[:, c, :], bv_rep[:, c, :], ident_f32[:])
@@ -148,11 +144,14 @@ def tile_graphditunit_pa_kernel(
         nc.vector.tensor_tensor(
             out=add[:], in0=bv_all[:].rearrange("p c n -> p (c n)"), in1=mul[:], op=ALU.mult
         )
+        nc.vector.tensor_tensor(out=add[:], in0=add[:], in1=shift_gate[:], op=ALU.add)
+
+        for r in range(EARLY_ROUNDS, ROUNDS):
+            transpose_x(r)
 
         x_codes = []
         x_scales = []
-
-        def quantise_x(r):
+        for r in range(ROUNDS):
             codes_r = per_round.tile([P, ROWS * B], U32, align_bytes=64)
             scales_r = per_round.tile([P, ROWS * B], U8, align_bytes=64)
             nc.vector.quantize_mx(
@@ -160,14 +159,6 @@ def tile_graphditunit_pa_kernel(
             )
             x_codes.append(codes_r)
             x_scales.append(scales_r)
-
-        quantise_x(0)
-        nc.vector.tensor_tensor(out=add[:], in0=add[:], in1=shift_gate[:], op=ALU.add)
-
-        for r in range(EARLY_ROUNDS, ROUNDS):
-            transpose_x(r)
-        for r in range(1, ROUNDS):
-            quantise_x(r)
 
         add_t_psum = psum.tile([P, CHUNKS, B], F32, tag="bank")
         for c in range(CHUNKS):

from contextlib import ExitStack

import concourse.mybir as mybir
from concourse.masks import make_identity

F32 = mybir.dt.float32
BF16 = mybir.dt.bfloat16
U32 = mybir.dt.uint32
U8 = mybir.dt.uint8
FP8X4 = mybir.dt.float8_e4m3fn_x4
ACT = mybir.ActivationFunctionType
ALU = mybir.AluOpType

P = 128
B, S, D, DO, E = 128, 16, 512, 512, 128
PACK = 4
HALVES = 2
ROWS = 2
ROUNDS = S // ROWS
CHUNKS = DO // P
RUN = 4
EARLY_ROUNDS = 2
ADD_LAG = 3

FLOPS = 2 * B * S * D * DO + 3 * 2 * B * E * DO


def tile_graphditunit_pa_kernel(
    tc, x, edge_features, Wv, bv, Wgate, bgate, Wscale, bscale, Wshift, bshift, out
):
    nc = tc.nc
    with ExitStack() as ctx:
        ctx.enter_context(tc.manual_schedule())
        const = ctx.enter_context(tc.tile_pool(name="const", bufs=1))
        per_round = ctx.enter_context(tc.tile_pool(name="per_round", bufs=ROUNDS))
        per_row = ctx.enter_context(tc.tile_pool(name="per_row", bufs=S))
        psum_add = ctx.enter_context(tc.psum_pool(name="psum_add", bufs=1))
        psum = ctx.enter_context(tc.psum_pool(name="psum", bufs=7))

        ident_bf16 = const.tile([P, P], BF16)
        make_identity(nc, ident_bf16[:])
        ident_f32 = const.tile([P, P], F32)
        make_identity(nc, ident_f32[:])
        bv_rows = const.tile([P, P], BF16)
        nc.vector.memset(bv_rows[:], 0.0)
        nc.scalar.dma_start(out=bv_rows[0:CHUNKS, :], in_=bv.rearrange("(c n) -> c n", n=P))
        bias_planes = []
        for bias in (bgate, bscale, bshift):
            plane = const.tile([P, DO], BF16, tag="plane", bufs=3)
            nc.vector.memset(plane[:], 0.0)
            nc.scalar.dma_start(out=plane[0:1, :], in_=bias.rearrange("(o c) -> o c", o=1))
            bias_planes.append(plane)
        ones = const.tile([P, P], BF16)
        nc.vector.memset(ones[:], 1.0)
        warm = const.tile([P, 1], F32)
        nc.vector.memset(warm[:], 0.0)
        nc.scalar.activation(out=warm[:], in_=warm[:], func=ACT.Sigmoid)

        e_sb = const.tile([P, E], BF16)
        nc.sync.dma_start(out=e_sb[:], in_=edge_features)
        w_mod = const.tile([P, 3, DO], BF16)
        nc.sync.dma_start(out=w_mod[:, 0, :], in_=Wgate)
        nc.sync.dma_start(out=w_mod[:, 1, :], in_=Wscale)
        w_raw = const.tile([P, PACK, DO], BF16)
        nc.sync.dma_start(
            out=w_raw[:].rearrange("p (u e) c -> p u (e c)", u=HALVES),
            in_=Wv.rearrange("(u p e) c -> p u (e c)", u=HALVES, p=P),
        )
        nc.sync.dma_start(out=w_mod[:, 2, :], in_=Wshift)
        x_tiles = []
        for r in range(ROUNDS):
            x_r = per_round.tile([P, ROWS * D], BF16)
            nc.sync.dma_start(
                out=x_r[:], in_=x[:, r * ROWS : (r + 1) * ROWS, :].rearrange("b i k -> b (i k)")
            )
            x_tiles.append(x_r)

        small_t = psum.tile([P, 2, P], BF16, tag="bank")
        nc.tensor.transpose(small_t[:, 0, :], e_sb[:], ident_bf16[:])
        nc.tensor.transpose(small_t[:, 1, :], bv_rows[:], ident_bf16[:])
        e_t = const.tile([P, B], BF16)
        nc.vector.tensor_copy(out=e_t[:], in_=small_t[:, 0, :])
        bv_t = const.tile([P, CHUNKS], F32)
        nc.vector.tensor_copy(out=bv_t[:], in_=small_t[:, 1, 0:CHUNKS])
        bv_rep = const.tile([P, CHUNKS, P], F32)
        nc.vector.tensor_copy(out=bv_rep[:], in_=bv_t[:].unsqueeze(2).to_broadcast([P, CHUNKS, P]))

        def edge_matmul(j):
            pre_j = psum.tile([P, DO], F32, tag="bank")
            nc.tensor.matmul(out=pre_j[:], lhsT=e_t[:], rhs=w_mod[:, j, :], start=True, stop=False)
            nc.tensor.matmul(out=pre_j[:], lhsT=ones[:], rhs=bias_planes[j][:], start=False, stop=True)
            return pre_j

        pre_gate = edge_matmul(0)
        gate = const.tile([P, DO], F32)
        nc.scalar.activation(out=gate[:], in_=pre_gate[:], func=ACT.Sigmoid)
        pre_scale = edge_matmul(1)
        scale = const.tile([P, DO], F32)
        nc.scalar.activation(out=scale[:], in_=pre_scale[:], func=ACT.Tanh)

        w_grouped = const.tile([P, DO, PACK], BF16, align_bytes=64)
        nc.vector.tensor_copy(
            out=w_grouped[:].rearrange("p (c i) t -> p c t i", i=RUN),
            in_=w_raw[:].rearrange("p t (c i) -> p c t i", i=RUN),
        )
        w_codes = const.tile([P, DO], U32, align_bytes=64)
        w_scales = const.tile([P, DO], U8, align_bytes=64)
        nc.vector.quantize_mx(
            out=w_codes[:].bitcast(FP8X4),
            scales=w_scales[:],
            in_=w_grouped[:].rearrange("p c t -> p (c t)"),
        )

        x_grouped = []

        def transpose_x(r):
            x_words = x_tiles[r][:].bitcast(F32)
            x_t = psum.tile([P, ROWS, HALVES, B], F32, tag="bank")
            for i in range(ROWS):
                for u in range(HALVES):
                    first = (i * HALVES + u) * P
                    nc.tensor.transpose(x_t[:, i, u, :], x_words[:, first : first + P], ident_f32[:])
            grouped_r = per_round.tile([P, ROWS * B * PACK], BF16, align_bytes=64)
            nc.scalar.copy(
                out=grouped_r[:].bitcast(F32).rearrange("p (i b u) -> p i b u", i=ROWS, u=HALVES),
                in_=x_t[:].rearrange("p i u b -> p i b u"),
            )
            x_grouped.append(grouped_r)

        for r in range(EARLY_ROUNDS):
            transpose_x(r)

        shift = edge_matmul(2)
        bv_all = psum.tile([P, CHUNKS, P], F32, tag="bank")
        for c in range(CHUNKS):
            nc.tensor.transpose(bv_all[:, c, :], bv_rep[:, c, :], ident_f32[:])
        mul = const.tile([P, DO], F32)
        nc.vector.scalar_tensor_tensor(
            out=mul[:], in0=scale[:], scalar=1.0, in1=gate[:], op0=ALU.add, op1=ALU.mult
        )
        shift_gate = const.tile([P, DO], F32)
        nc.vector.tensor_tensor(out=shift_gate[:], in0=shift[:], in1=gate[:], op=ALU.mult)
        add = const.tile([P, DO], F32)
        nc.vector.tensor_tensor(
            out=add[:], in0=bv_all[:].rearrange("p c n -> p (c n)"), in1=mul[:], op=ALU.mult
        )
        nc.vector.tensor_tensor(out=add[:], in0=add[:], in1=shift_gate[:], op=ALU.add)

        for r in range(EARLY_ROUNDS, ROUNDS):
            transpose_x(r)

        x_codes = []
        x_scales = []
        for r in range(ROUNDS):
            codes_r = per_round.tile([P, ROWS * B], U32, align_bytes=64)
            scales_r = per_round.tile([P, ROWS * B], U8, align_bytes=64)
            nc.vector.quantize_mx(
                out=codes_r[:].bitcast(FP8X4), scales=scales_r[:], in_=x_grouped[r][:]
            )
            x_codes.append(codes_r)
            x_scales.append(scales_r)

        add_t_psum = psum.tile([P, CHUNKS, B], F32, tag="bank")
        for c in range(CHUNKS):
            nc.tensor.transpose(add_t_psum[:, c, :], add[:, c * P : (c + 1) * P], ident_f32[:])
        add_t = const.tile([P, CHUNKS, B], F32)
        nc.scalar.copy(out=add_t[:], in_=add_t_psum[:])

        products = []

        def multiply(i):
            r = i // ROWS
            samples = slice((i % ROWS) * B, (i % ROWS + 1) * B)
            acc = psum.tile([P, DO], F32, tag="bank")
            nc.tensor.matmul_mx(
                out=acc[:],
                lhsT=x_codes[r][:, samples].bitcast(FP8X4),
                lhsT_scale=x_scales[r][:, samples],
                rhs=w_codes[:].bitcast(FP8X4),
                rhs_scale=w_scales[:],
                start=True,
                stop=True,
            )
            o_i = per_row.tile([P, DO], F32)
            nc.vector.tensor_tensor(out=o_i[:], in0=acc[:], in1=mul[:], op=ALU.mult)
            products.append(o_i)

        def add_and_store(i):
            o_i = products[i]
            if i % 2 == 0:
                nc.gpsimd.tensor_tensor(out=o_i[:], in0=o_i[:], in1=add[:], op=ALU.add)
            else:
                nc.vector.tensor_tensor(
                    out=o_i[:], in0=o_i[:], in1=add_psum[:].rearrange("p c n -> p (c n)"), op=ALU.add
                )
            nc.sync.dma_start(out=out[:, i, :], in_=o_i[:])

        for i in range(ADD_LAG):
            multiply(i)
        add_psum = psum_add.tile([P, CHUNKS, P], F32)
        for c in range(CHUNKS):
            nc.tensor.transpose(add_psum[:, c, :], add_t[:, c, :], ident_f32[:])
        for i in range(ADD_LAG, S):
            multiply(i)
            add_and_store(i - ADD_LAG)
        for i in range(S - ADD_LAG, S):
            add_and_store(i)
